import numpy as np
import ml_dtypes


def mxq(x, axis, fmt="e4m3"):
    dtype, down = {"e4m3": (ml_dtypes.float8_e4m3fn, 7), "e5m2": (ml_dtypes.float8_e5m2, 14)}[fmt]
    v = np.moveaxis(np.asarray(x, np.float32).astype(ml_dtypes.bfloat16).astype(np.float64), axis, -1)
    blocks = v.reshape(v.shape[:-1] + (-1, 32))
    amax = np.abs(blocks).max(-1, keepdims=True)
    byte = np.maximum(np.where(amax > 0, np.frexp(amax)[1] - 1 + 127, 0) - down, 1)
    scale = np.exp2(byte - 127.0)
    codes = (blocks / scale).astype(np.float32).astype(dtype).astype(np.float64)
    return np.moveaxis((codes * scale).reshape(v.shape), -1, axis)


WIDE = False


def mx_kscale(k):
    if not WIDE:
        return np.ones(k)
    levels = np.array([10, -10, 5, -5, 0])
    a = np.random.permutation(np.resize(levels, k // 512 * 4)).reshape(k // 512, 4)
    idx = np.arange(k)
    return np.exp2(a[idx // 512, idx % 128 // 32])


BF16 = ml_dtypes.bfloat16


def bf(x):
    return np.asarray(x, np.float32).astype(BF16)


def f64(x):
    return np.asarray(x).astype(np.float64)


B, HW, C, HID, WS, SS, HEADS = 1, 32, 1024, 2048, 8, 4, 16
L = HW * HW
NH = HW // WS
HD = C // HEADS
EPS = 1e-5


def ln(x, w, b):
    m = x.mean(-1, keepdims=True)
    xm = x - m
    v = np.mean(xm * xm, axis=-1, keepdims=True)
    return xm * (1.0 / np.sqrt(v + EPS)) * w + b


def setup_inputs():
    s = mx_kscale(C)
    return {"x": bf(np.random.standard_normal((B, L, C))),
            "ln1_w": bf((1.0 + 0.1 * np.random.standard_normal(C)) * s),
            "ln1_b": bf(0.1 * np.random.standard_normal(C) * s),
            "in_proj_w": bf(np.random.standard_normal((3 * C, C)) / np.sqrt(C) / s[None, :]),
            "in_proj_b": bf(0.1 * np.random.standard_normal(3 * C))}


def reference(x, ln1_w, ln1_b, in_proj_w, in_proj_b):
    h = ln(f64(x), f64(ln1_w), f64(ln1_b)).reshape(B, HW, HW, C)
    h = np.roll(h, (-SS, -SS), axis=(1, 2))
    win = np.swapaxes(h.reshape(B, NH, WS, NH, WS, C), 2, 3).reshape(-1, WS * WS, C)
    win = win
    qkv = (mxq(win, 2, "e4m3") @ mxq(f64(in_proj_w), 1, "e4m3").T) + f64(in_proj_b)
    q, k, v = np.split(qkv, 3, axis=-1)
    S, N = win.shape[0], win.shape[1]
    q = q.reshape(S, N, HEADS, HD) * (HD ** -0.5)
    k = k.reshape(S, N, HEADS, HD)
    v = v.reshape(S, N, HEADS, HD)
    return q, k, v

@@ -1,0 +1,264 @@
+from contextlib import ExitStack
+
+import concourse.mybir as mybir
+from concourse.masks import make_identity
+
+F32 = mybir.dt.float32
+BF16 = mybir.dt.bfloat16
+U32 = mybir.dt.uint32
+U8 = mybir.dt.uint8
+FP8X4 = mybir.dt.float8_e4m3fn_x4
+ALU = mybir.AluOpType
+ACT = mybir.ActivationFunctionType
+
+P = 128
+TOKENS = 1024
+CHANNELS = 1024
+OUT_COLS = 3072
+GRID = 32
+SHIFT = 4
+WINDOW = 8
+WINDOWS_IN_ROW = GRID // WINDOW
+GRID_ROWS_IN_TILE = P // GRID
+EPS = 1e-5
+Q_SCALE = 64 ** -0.5
+
+PACK = 4
+K_PASS = P * PACK
+PASSES = CHANNELS // K_PASS
+BANK = 512
+W_BLOCKS = OUT_COLS // BANK
+W_TILES = BANK // P
+X_TILES = TOKENS // P
+HALVES = 2
+HALF_TILES = X_TILES // HALVES
+PLANES = CHANNELS // P
+BN_CHUNK = 512
+
+FLOPS = 2 * TOKENS * CHANNELS * OUT_COLS
+
+
+def tile_swintransformerblock_pa_kernel(
+    tc, x, ln1_w, ln1_b, in_proj_w, in_proj_b, out_0, out_1, out_2
+):
+    nc = tc.nc
+    x_rows = x.flatten_outer_dims()
+    out_rows = [o.rearrange("w n h d -> (w n) (h d)") for o in (out_0, out_1, out_2)]
+
+    with ExitStack() as stack:
+        const = stack.enter_context(tc.tile_pool(name="const", bufs=1))
+        keep = stack.enter_context(tc.tile_pool(name="keep", bufs=1))
+        small = stack.enter_context(tc.tile_pool(name="small", bufs=4))
+        normed = stack.enter_context(tc.tile_pool(name="normed", bufs=HALF_TILES))
+        group_h = stack.enter_context(tc.tile_pool(name="group_h", bufs=2))
+        group_w = stack.enter_context(tc.tile_pool(name="group_w", bufs=3))
+        results = stack.enter_context(tc.tile_pool(name="results", bufs=8))
+        psum = stack.enter_context(tc.psum_pool(name="psum", bufs=8))
+
+        x_sb = [keep.tile([P, CHANNELS], BF16, name="x_sb%d" % s) for s in range(X_TILES)]
+        w_raw = [keep.tile([P, W_TILES, CHANNELS], BF16, name="w_raw%d" % n) for n in range(W_BLOCKS)]
+
+        def source_tile(shifted_tile):
+            return (shifted_tile + 1) % X_TILES
+
+        def load_x(half):
+            for i in range(HALF_TILES):
+                s = source_tile(half * HALF_TILES + i)
+                nc.sync.dma_start(out=x_sb[s][:], in_=x_rows[s * P : (s + 1) * P, :])
+
+        def load_w(n):
+            rows = in_proj_w[n * BANK : (n + 1) * BANK, :]
+            nc.sync.dma_start(out=w_raw[n][:], in_=rows.rearrange("(a p) k -> p a k", p=P))
+
+        load_x(0)
+        load_w(0)
+        load_x(1)
+        for n in range(1, W_BLOCKS):
+            load_w(n)
+
+        b_rows = const.tile([P, OUT_COLS], BF16)
+        nc.vector.memset(b_rows[:], 0.0)
+        nc.scalar.dma_start(out=b_rows[0:1, :], in_=in_proj_b.unsqueeze(0))
+        ln_gain_bf = const.tile([P, PLANES // 2, 2], BF16)
+        ln_bias_bf = const.tile([P, PLANES // 2, 2], BF16)
+        nc.scalar.dma_start(out=ln_gain_bf[:], in_=ln1_w.rearrange("(r p e) -> p r e", p=P, e=2))
+        nc.scalar.dma_start(out=ln_bias_bf[:], in_=ln1_b.rearrange("(r p e) -> p r e", p=P, e=2))
+        ln_gain = const.tile([P, PLANES // 2, 2], F32)
+        ln_bias = const.tile([P, PLANES // 2, 2], F32)
+        nc.vector.tensor_copy(out=ln_gain[:], in_=ln_gain_bf[:])
+        nc.vector.tensor_copy(out=ln_bias[:], in_=ln_bias_bf[:])
+
+        eps = const.tile([P, 1], F32)
+        eps_root = const.tile([P, 1], F32)
+        nc.vector.memset(eps[:], EPS)
+        nc.scalar.activation(out=eps_root[:], in_=eps[:], func=ACT.Sqrt)
+
+        ident = const.tile([P, P], F32)
+        make_identity(nc, ident[:])
+        ident_rows = ident[:].rearrange("p (i j) -> p i j", j=GRID)
+        rotated = const.tile([P, GRID_ROWS_IN_TILE, GRID], F32)
+        nc.vector.tensor_copy(out=rotated[:, :, 0 : GRID - SHIFT], in_=ident_rows[:, :, SHIFT:GRID])
+        nc.vector.tensor_copy(out=rotated[:, :, GRID - SHIFT : GRID], in_=ident_rows[:, :, 0:SHIFT])
+        perm = const.tile([P, WINDOWS_IN_ROW, GRID_ROWS_IN_TILE, WINDOW], F32)
+        nc.vector.tensor_copy(out=perm[:], in_=rotated[:].rearrange("p i (w c) -> p w i c", c=WINDOW))
+        perm_2d = perm[:].rearrange("p w i c -> p (w i c)")
+
+        def out_scale(n):
+            return Q_SCALE if n * BANK < CHANNELS else 1.0
+
+        ones = const.tile([P, P], BF16)
+        nc.vector.memset(ones[:], 1.0)
+        bias = const.tile([P, OUT_COLS], F32)
+        for n in range(W_BLOCKS):
+            cols = slice(n * BANK, (n + 1) * BANK)
+            spread = psum.tile([P, BANK], F32, tag="bank")
+            nc.tensor.matmul(out=spread[:], lhsT=ones[:], rhs=b_rows[:, cols], start=True, stop=True)
+            nc.scalar.mul(out=bias[:, cols], in_=spread[:], mul=out_scale(n))
+
+        h_codes = keep.tile([P, PASSES, TOKENS], U32, align_bytes=64)
+        h_scales = keep.tile([P, PASSES, TOKENS], U8, align_bytes=64)
+        w_codes = keep.tile([P, W_BLOCKS, PASSES, BANK], U32, align_bytes=64)
+        w_scales = keep.tile([P, W_BLOCKS, PASSES, BANK], U8, align_bytes=64)
+        planes = [keep.tile([P, PLANES, BANK], BF16, name="planes%d" % h) for h in range(HALVES)]
+        xn = {}
+        grouped_w = {}
+
+        def normalise(half):
+            for i in range(HALF_TILES):
+                s = source_tile(half * HALF_TILES + i)
+                stats = small.tile([P, CHANNELS // BN_CHUNK, 6], F32, tag="stats")
+                for c in range(CHANNELS // BN_CHUNK):
+                    nc.vector.bn_stats(out=stats[:, c, :], in_=x_sb[s][:, c * BN_CHUNK : (c + 1) * BN_CHUNK])
+                mean_var = small.tile([P, 2], F32, tag="mean_var")
+                nc.vector.bn_aggr(out=mean_var[:], in_=stats[:].rearrange("p c s -> p (c s)"))
+                std = small.tile([P, 1], F32, tag="std")
+                nc.scalar.activation(out=std[:], in_=mean_var[:, 1:2], func=ACT.Sqrt, bias=eps[:, 0:1])
+                neg_mean = small.tile([P, 1], F32, tag="neg_mean")
+                nc.vector.tensor_scalar_mul(out=neg_mean[:], in0=mean_var[:, 0:1], scalar1=-1.0)
+                rstd = small.tile([P, 1], F32, tag="rstd")
+                nc.vector.reciprocal(out=rstd[:], in_=std[:])
+                xn[s] = normed.tile([P, 2, CHANNELS // 2], F32, name="xn", tag="xn")
+                nc.gpsimd.tensor_scalar(
+                    out=xn[s][:],
+                    in0=x_sb[s][:].rearrange("p (w e) -> p e w", e=2),
+                    scalar1=neg_mean[:, 0:1],
+                    scalar2=rstd[:, 0:1],
+                    op0=ALU.add,
+                    op1=ALU.mult,
+                )
+
+        def turn_h(half, g):
+            banks = [
+                psum.tile([P, 2, WINDOWS_IN_ROW, 2, P // WINDOWS_IN_ROW], F32, name="turned_h", tag="bank")
+                for t in range(PACK)
+            ]
+            for i in range(HALF_TILES):
+                wr, hb = divmod(i, 2)
+                s = source_tile(half * HALF_TILES + i)
+                for t in range(PACK):
+                    r, e = divmod(PACK * g + t, 2)
+                    nc.tensor.transpose(
+                        out=banks[t][:, wr, :, hb, :], in_=xn[s][:, e, r * P : (r + 1) * P], identity=perm_2d
+                    )
+            for t in range(PACK):
+                r, e = divmod(PACK * g + t, 2)
+                nc.scalar.activation(
+                    out=planes[half][:, PACK * g + t, :],
+                    in_=banks[t][:].rearrange("p a w b c -> p (a w b c)"),
+                    func=ACT.Identity,
+                    scale=ln_gain[:, r, e : e + 1],
+                    bias=ln_bias[:, r, e : e + 1],
+                )
+
+        def quantise_h(half, g):
+            rows = slice(half * BANK, (half + 1) * BANK)
+            grouped = group_h.tile([P, BANK, PACK], BF16, align_bytes=64, tag="grouped_h")
+            nc.vector.tensor_copy(
+                out=grouped[:], in_=planes[half][:, PACK * g : PACK * (g + 1), :].rearrange("p t c -> p c t")
+            )
+            nc.vector.quantize_mx(
+                out=h_codes[:, g, rows].bitcast(FP8X4),
+                scales=h_scales[:, g, rows],
+                in_=grouped[:].rearrange("p c t -> p (c t)"),
+            )
+
+        def turn_w(n):
+            words = w_raw[n][:].bitcast(F32)
+            for g in range(PASSES):
+                grouped_w[n, g] = group_w.tile([P, BANK, PACK], BF16, align_bytes=64, name="grouped_w", tag="grouped_w")
+                grouped_words = grouped_w[n, g][:].bitcast(F32)
+                for pair in range(W_TILES // 2):
+                    turned = psum.tile([P, 2, 2, P], F32, tag="bank")
+                    for u in range(2):
+                        for a2 in range(2):
+                            first = (2 * g + u) * P
+                            nc.tensor.transpose(
+                                out=turned[:, u, a2, :],
+                                in_=words[:, 2 * pair + a2, first : first + P],
+                                identity=ident[:],
+                            )
+                    nc.scalar.copy(
+                        out=grouped_words[:, 2 * pair * P : 2 * (pair + 1) * P, :],
+                        in_=turned[:].rearrange("p u a c -> p (a c) u"),
+                    )
+
+        def quantise_w(n):
+            for g in range(PASSES):
+                nc.vector.quantize_mx(
+                    out=w_codes[:, n, g, :].bitcast(FP8X4),
+                    scales=w_scales[:, n, g, :],
+                    in_=grouped_w[n, g][:].rearrange("p c t -> p (c t)"),
+                )
+
+        result_of = {}
+
+        def project(half, n):
+            cols = slice(n * BANK, (n + 1) * BANK)
+            which, part = divmod(n, CHANNELS // BANK)
+            part_cols = slice(part * BANK, (part + 1) * BANK)
+            for i in range(HALF_TILES):
+                m = half * HALF_TILES + i
+                rows = slice(m * P, (m + 1) * P)
+                acc = psum.tile([P, BANK], F32, tag="bank")
+                for g in range(PASSES):
+                    nc.tensor.matmul_mx(
+                        out=acc[:],
+                        lhsT=h_codes[:, g, rows].bitcast(FP8X4),
+                        lhsT_scale=h_scales[:, g, rows],
+                        rhs=w_codes[:, n, g, :].bitcast(FP8X4),
+                        rhs_scale=w_scales[:, n, g, :],
+                        start=(g == 0),
+                        stop=(g == PASSES - 1),
+                    )
+                if part == 0:
+                    result_of[m] = results.tile([P, CHANNELS], F32, name="result", tag="result")
+                result = result_of[m][:, part_cols]
+                if (n * HALF_TILES + i) % 3 == 2:
+                    nc.scalar.mul(out=result, in_=acc[:], mul=out_scale(n))
+                    nc.gpsimd.tensor_tensor(out=result, in0=result, in1=bias[:, cols], op=ALU.add)
+                else:
+                    nc.vector.scalar_tensor_tensor(
+                        out=result, in0=acc[:], scalar=out_scale(n), in1=bias[:, cols], op0=ALU.mult, op1=ALU.add
+                    )
+                if part == CHANNELS // BANK - 1:
+                    nc.sync.dma_start(out=out_rows[which][rows, :], in_=result_of[m][:])
+
+        normalise(0)
+        turn_w(0)
+        quantise_w(0)
+        for g in range(PASSES):
+            turn_h(0, g)
+            quantise_h(0, g)
+        turn_w(1)
+        quantise_w(1)
+        normalise(1)
+        for n in range(W_BLOCKS):
+            if n + 2 < W_BLOCKS:
+                turn_w(n + 2)
+                quantise_w(n + 2)
+            if n in (2, 3):
+                turn_h(1, n - 2)
+                quantise_h(1, n - 2)
+            project(0, n)
+        for n in range(W_BLOCKS):
+            project(1, n)

@@ -46,29 +46,38 @@ def tile_swintransformerblock_pa_kernel(
     out_rows = [o.rearrange("w n h d -> (w n) (h d)") for o in (out_0, out_1, out_2)]
 
     with ExitStack() as stack:
+        stack.enter_context(tc.manual_schedule())
         const = stack.enter_context(tc.tile_pool(name="const", bufs=1))
         keep = stack.enter_context(tc.tile_pool(name="keep", bufs=1))
-        small = stack.enter_context(tc.tile_pool(name="small", bufs=4))
-        normed = stack.enter_context(tc.tile_pool(name="normed", bufs=HALF_TILES))
+        small = stack.enter_context(tc.tile_pool(name="small", bufs=X_TILES))
+        normed = stack.enter_context(tc.tile_pool(name="normed", bufs=6))
         group_h = stack.enter_context(tc.tile_pool(name="group_h", bufs=2))
-        group_w = stack.enter_context(tc.tile_pool(name="group_w", bufs=3))
+        group_w = stack.enter_context(tc.tile_pool(name="group_w", bufs=4))
         results = stack.enter_context(tc.tile_pool(name="results", bufs=8))
         psum = stack.enter_context(tc.psum_pool(name="psum", bufs=8))
 
         x_sb = [keep.tile([P, CHANNELS], BF16, name="x_sb%d" % s) for s in range(X_TILES)]
         w_raw = [keep.tile([P, W_TILES, CHANNELS], BF16, name="w_raw%d" % n) for n in range(W_BLOCKS)]
 
-        def source_tile(shifted_tile):
-            return (shifted_tile + 1) % X_TILES
+        def source_tile(half, i):
+            return (half * HALF_TILES + i + 1) % X_TILES
 
         def load_x(half):
             for i in range(HALF_TILES):
-                s = source_tile(half * HALF_TILES + i)
+                s = source_tile(half, i)
                 nc.sync.dma_start(out=x_sb[s][:], in_=x_rows[s * P : (s + 1) * P, :])
 
         def load_w(n):
             rows = in_proj_w[n * BANK : (n + 1) * BANK, :]
             nc.sync.dma_start(out=w_raw[n][:], in_=rows.rearrange("(a p) k -> p a k", p=P))
+
+        ln_gain_bf = const.tile([P, PLANES // 2, 2], BF16)
+        ln_bias_bf = const.tile([P, PLANES // 2, 2], BF16)
+        nc.scalar.dma_start(out=ln_gain_bf[:], in_=ln1_w.rearrange("(r p e) -> p r e", p=P, e=2))
+        nc.scalar.dma_start(out=ln_bias_bf[:], in_=ln1_b.rearrange("(r p e) -> p r e", p=P, e=2))
+        b_rows = const.tile([P, OUT_COLS], BF16)
+        nc.vector.memset(b_rows[:], 0.0)
+        nc.scalar.dma_start(out=b_rows[0:1, :], in_=in_proj_b.unsqueeze(0))
 
         load_x(0)
         load_w(0)
@@ -76,22 +85,12 @@ def tile_swintransformerblock_pa_kernel(
         for n in range(1, W_BLOCKS):
             load_w(n)
 
-        b_rows = const.tile([P, OUT_COLS], BF16)
-        nc.vector.memset(b_rows[:], 0.0)
-        nc.scalar.dma_start(out=b_rows[0:1, :], in_=in_proj_b.unsqueeze(0))
-        ln_gain_bf = const.tile([P, PLANES // 2, 2], BF16)
-        ln_bias_bf = const.tile([P, PLANES // 2, 2], BF16)
-        nc.scalar.dma_start(out=ln_gain_bf[:], in_=ln1_w.rearrange("(r p e) -> p r e", p=P, e=2))
-        nc.scalar.dma_start(out=ln_bias_bf[:], in_=ln1_b.rearrange("(r p e) -> p r e", p=P, e=2))
-        ln_gain = const.tile([P, PLANES // 2, 2], F32)
-        ln_bias = const.tile([P, PLANES // 2, 2], F32)
-        nc.vector.tensor_copy(out=ln_gain[:], in_=ln_gain_bf[:])
-        nc.vector.tensor_copy(out=ln_bias[:], in_=ln_bias_bf[:])
-
         eps = const.tile([P, 1], F32)
-        eps_root = const.tile([P, 1], F32)
+        eps_rsqrt = const.tile([P, 1], F32)
         nc.vector.memset(eps[:], EPS)
-        nc.scalar.activation(out=eps_root[:], in_=eps[:], func=ACT.Sqrt)
+        nc.scalar.activation(out=eps_rsqrt[:], in_=eps[:], func=ACT.Abs_reciprocal_sqrt)
+        ones = const.tile([P, P], BF16)
+        nc.vector.memset(ones[:], 1.0)
 
         ident = const.tile([P, P], F32)
         make_identity(nc, ident[:])
@@ -102,14 +101,17 @@ def tile_swintransformerblock_pa_kernel(
         perm = const.tile([P, WINDOWS_IN_ROW, GRID_ROWS_IN_TILE, WINDOW], F32)
         nc.vector.tensor_copy(out=perm[:], in_=rotated[:].rearrange("p i (w c) -> p w i c", c=WINDOW))
         perm_2d = perm[:].rearrange("p w i c -> p (w i c)")
+        ln_gain = const.tile([P, PLANES // 2, 2], F32)
+        ln_bias = const.tile([P, PLANES // 2, 2], F32)
+        nc.gpsimd.tensor_copy(out=ln_gain[:], in_=ln_gain_bf[:])
+        nc.gpsimd.tensor_copy(out=ln_bias[:], in_=ln_bias_bf[:])
 
         def out_scale(n):
             return Q_SCALE if n * BANK < CHANNELS else 1.0
 
-        ones = const.tile([P, P], BF16)
-        nc.vector.memset(ones[:], 1.0)
         bias = const.tile([P, OUT_COLS], F32)
-        for n in range(W_BLOCKS):
+
+        def spread_bias(n):
             cols = slice(n * BANK, (n + 1) * BANK)
             spread = psum.tile([P, BANK], F32, tag="bank")
             nc.tensor.matmul(out=spread[:], lhsT=ones[:], rhs=b_rows[:, cols], start=True, stop=True)
@@ -120,51 +122,49 @@ def tile_swintransformerblock_pa_kernel(
         w_codes = keep.tile([P, W_BLOCKS, PASSES, BANK], U32, align_bytes=64)
         w_scales = keep.tile([P, W_BLOCKS, PASSES, BANK], U8, align_bytes=64)
         planes = [keep.tile([P, PLANES, BANK], BF16, name="planes%d" % h) for h in range(HALVES)]
+        mean_var = {}
+        neg_mean = {}
         xn = {}
         grouped_w = {}
 
-        def normalise(half):
-            for i in range(HALF_TILES):
-                s = source_tile(half * HALF_TILES + i)
-                stats = small.tile([P, CHANNELS // BN_CHUNK, 6], F32, tag="stats")
-                for c in range(CHANNELS // BN_CHUNK):
-                    nc.vector.bn_stats(out=stats[:, c, :], in_=x_sb[s][:, c * BN_CHUNK : (c + 1) * BN_CHUNK])
-                mean_var = small.tile([P, 2], F32, tag="mean_var")
-                nc.vector.bn_aggr(out=mean_var[:], in_=stats[:].rearrange("p c s -> p (c s)"))
-                std = small.tile([P, 1], F32, tag="std")
-                nc.scalar.activation(out=std[:], in_=mean_var[:, 1:2], func=ACT.Sqrt, bias=eps[:, 0:1])
-                neg_mean = small.tile([P, 1], F32, tag="neg_mean")
-                nc.vector.tensor_scalar_mul(out=neg_mean[:], in0=mean_var[:, 0:1], scalar1=-1.0)
-                rstd = small.tile([P, 1], F32, tag="rstd")
-                nc.vector.reciprocal(out=rstd[:], in_=std[:])
-                xn[s] = normed.tile([P, 2, CHANNELS // 2], F32, name="xn", tag="xn")
-                nc.gpsimd.tensor_scalar(
-                    out=xn[s][:],
-                    in0=x_sb[s][:].rearrange("p (w e) -> p e w", e=2),
-                    scalar1=neg_mean[:, 0:1],
-                    scalar2=rstd[:, 0:1],
-                    op0=ALU.add,
-                    op1=ALU.mult,
-                )
+        def tile_stats(s):
+            stats = small.tile([P, CHANNELS // BN_CHUNK, 6], F32, tag="stats")
+            for c in range(CHANNELS // BN_CHUNK):
+                nc.vector.bn_stats(out=stats[:, c, :], in_=x_sb[s][:, c * BN_CHUNK : (c + 1) * BN_CHUNK])
+            mean_var[s] = small.tile([P, 2], F32, name="mean_var", tag="mean_var")
+            nc.vector.bn_aggr(out=mean_var[s][:], in_=stats[:].rearrange("p c s -> p (c s)"))
+            neg_mean[s] = small.tile([P, 1], F32, name="neg_mean", tag="neg_mean")
+            nc.vector.tensor_scalar_mul(out=neg_mean[s][:], in0=mean_var[s][:, 0:1], scalar1=-1.0)
+
+        def tile_norm(s):
+            rstd = small.tile([P, 1], F32, tag="rstd")
+            nc.scalar.activation(
+                out=rstd[:], in_=mean_var[s][:, 1:2], func=ACT.Abs_reciprocal_sqrt, bias=eps[:, 0:1]
+            )
+            xn[s] = normed.tile([P, 2, CHANNELS // 2], F32, name="xn", tag="xn")
+            nc.gpsimd.tensor_scalar(
+                out=xn[s][:],
+                in0=x_sb[s][:].rearrange("p (w e) -> p e w", e=2),
+                scalar1=neg_mean[s][:, 0:1],
+                scalar2=rstd[:, 0:1],
+                op0=ALU.add,
+                op1=ALU.mult,
+            )
 
         def turn_h(half, g):
-            banks = [
-                psum.tile([P, 2, WINDOWS_IN_ROW, 2, P // WINDOWS_IN_ROW], F32, name="turned_h", tag="bank")
-                for t in range(PACK)
-            ]
-            for i in range(HALF_TILES):
-                wr, hb = divmod(i, 2)
-                s = source_tile(half * HALF_TILES + i)
-                for t in range(PACK):
-                    r, e = divmod(PACK * g + t, 2)
-                    nc.tensor.transpose(
-                        out=banks[t][:, wr, :, hb, :], in_=xn[s][:, e, r * P : (r + 1) * P], identity=perm_2d
-                    )
             for t in range(PACK):
                 r, e = divmod(PACK * g + t, 2)
+                turned = psum.tile([P, 2, WINDOWS_IN_ROW, 2, P // WINDOWS_IN_ROW], F32, tag="bank")
+                for i in range(HALF_TILES):
+                    wr, hb = divmod(i, 2)
+                    nc.tensor.transpose(
+                        out=turned[:, wr, :, hb, :],
+                        in_=xn[source_tile(half, i)][:, e, r * P : (r + 1) * P],
+                        identity=perm_2d,
+                    )
                 nc.scalar.activation(
                     out=planes[half][:, PACK * g + t, :],
-                    in_=banks[t][:].rearrange("p a w b c -> p (a w b c)"),
+                    in_=turned[:].rearrange("p a w b c -> p (a w b c)"),
                     func=ACT.Identity,
                     scale=ln_gain[:, r, e : e + 1],
                     bias=ln_bias[:, r, e : e + 1],
@@ -216,13 +216,12 @@ def tile_swintransformerblock_pa_kernel(
             cols = slice(n * BANK, (n + 1) * BANK)
             which, part = divmod(n, CHANNELS // BANK)
             part_cols = slice(part * BANK, (part + 1) * BANK)
-            for i in range(HALF_TILES):
-                m = half * HALF_TILES + i
-                rows = slice(m * P, (m + 1) * P)
-                acc = psum.tile([P, BANK], F32, tag="bank")
-                for g in range(PASSES):
+            accs = [psum.tile([P, BANK], F32, name="acc", tag="bank") for i in range(HALF_TILES)]
+            for g in range(PASSES):
+                for i in range(HALF_TILES):
+                    rows = slice((half * HALF_TILES + i) * P, (half * HALF_TILES + i + 1) * P)
                     nc.tensor.matmul_mx(
-                        out=acc[:],
+                        out=accs[i][:],
                         lhsT=h_codes[:, g, rows].bitcast(FP8X4),
                         lhsT_scale=h_scales[:, g, rows],
                         rhs=w_codes[:, n, g, :].bitcast(FP8X4),
@@ -230,35 +229,52 @@ def tile_swintransformerblock_pa_kernel(
                         start=(g == 0),
                         stop=(g == PASSES - 1),
                     )
+            for i in range(HALF_TILES):
+                m = half * HALF_TILES + i
                 if part == 0:
                     result_of[m] = results.tile([P, CHANNELS], F32, name="result", tag="result")
                 result = result_of[m][:, part_cols]
                 if (n * HALF_TILES + i) % 3 == 2:
-                    nc.scalar.mul(out=result, in_=acc[:], mul=out_scale(n))
+                    nc.scalar.mul(out=result, in_=accs[i][:], mul=out_scale(n))
                     nc.gpsimd.tensor_tensor(out=result, in0=result, in1=bias[:, cols], op=ALU.add)
                 else:
                     nc.vector.scalar_tensor_tensor(
-                        out=result, in0=acc[:], scalar=out_scale(n), in1=bias[:, cols], op0=ALU.mult, op1=ALU.add
+                        out=result, in0=accs[i][:], scalar=out_scale(n), in1=bias[:, cols], op0=ALU.mult, op1=ALU.add
                     )
                 if part == CHANNELS // BANK - 1:
-                    nc.sync.dma_start(out=out_rows[which][rows, :], in_=result_of[m][:])
+                    nc.sync.dma_start(out=out_rows[which][m * P : (m + 1) * P, :], in_=result_of[m][:])
 
-        normalise(0)
+        for i in range(HALF_TILES):
+            tile_stats(source_tile(0, i))
+            tile_norm(source_tile(0, i))
+            for n in range(2 * i, min(2 * i + 2, W_BLOCKS)):
+                spread_bias(n)
         turn_w(0)
+        tile_stats(source_tile(1, 0))
+        tile_stats(source_tile(1, 1))
         quantise_w(0)
-        for g in range(PASSES):
-            turn_h(0, g)
-            quantise_h(0, g)
+        turn_h(0, 0)
+        tile_norm(source_tile(1, 0))
+        tile_norm(source_tile(1, 1))
+        tile_stats(source_tile(1, 2))
+        quantise_h(0, 0)
+        turn_h(0, 1)
+        tile_norm(source_tile(1, 2))
+        quantise_h(0, 1)
         turn_w(1)
         quantise_w(1)
-        normalise(1)
-        for n in range(W_BLOCKS):
-            if n + 2 < W_BLOCKS:
-                turn_w(n + 2)
-                quantise_w(n + 2)
-            if n in (2, 3):
-                turn_h(1, n - 2)
-                quantise_h(1, n - 2)
-            project(0, n)
+        turn_w(2)
+        project(0, 0)
+        quantise_w(2)
+        tile_stats(source_tile(1, 3))
+        tile_norm(source_tile(1, 3))
+        for n in range(3, W_BLOCKS):
+            turn_w(n)
+            quantise_w(n)
+            project(0, n - 2)
+        for g in range(PASSES):
+            turn_h(1, g)
+            quantise_h(1, g)
+            project(0, W_BLOCKS - PASSES + g)
         for n in range(W_BLOCKS):
             project(1, n)

@@ -34,6 +34,7 @@ HALVES = 2
 HALF_TILES = X_TILES // HALVES
 PLANES = CHANNELS // P
 BN_CHUNK = 512
+PARTS = CHANNELS // BANK
 
 FLOPS = 2 * TOKENS * CHANNELS * OUT_COLS
 
@@ -46,7 +47,6 @@ def tile_swintransformerblock_pa_kernel(
     out_rows = [o.rearrange("w n h d -> (w n) (h d)") for o in (out_0, out_1, out_2)]
 
     with ExitStack() as stack:
-        stack.enter_context(tc.manual_schedule())
         const = stack.enter_context(tc.tile_pool(name="const", bufs=1))
         keep = stack.enter_context(tc.tile_pool(name="keep", bufs=1))
         small = stack.enter_context(tc.tile_pool(name="small", bufs=X_TILES))
@@ -75,22 +75,21 @@ def tile_swintransformerblock_pa_kernel(
         ln_bias_bf = const.tile([P, PLANES // 2, 2], BF16)
         nc.scalar.dma_start(out=ln_gain_bf[:], in_=ln1_w.rearrange("(r p e) -> p r e", p=P, e=2))
         nc.scalar.dma_start(out=ln_bias_bf[:], in_=ln1_b.rearrange("(r p e) -> p r e", p=P, e=2))
-        b_rows = const.tile([P, OUT_COLS], BF16)
-        nc.vector.memset(b_rows[:], 0.0)
-        nc.scalar.dma_start(out=b_rows[0:1, :], in_=in_proj_b.unsqueeze(0))
 
         load_x(0)
         load_w(0)
         load_x(1)
-        for n in range(1, W_BLOCKS):
+        load_w(1)
+        load_w(2)
+        bias = const.tile([P, OUT_COLS], BF16)
+        nc.sync.dma_start(out=bias[:], in_=in_proj_b.partition_broadcast(P))
+        for n in range(3, W_BLOCKS):
             load_w(n)
 
         eps = const.tile([P, 1], F32)
         eps_rsqrt = const.tile([P, 1], F32)
         nc.vector.memset(eps[:], EPS)
         nc.scalar.activation(out=eps_rsqrt[:], in_=eps[:], func=ACT.Abs_reciprocal_sqrt)
-        ones = const.tile([P, P], BF16)
-        nc.vector.memset(ones[:], 1.0)
 
         ident = const.tile([P, P], F32)
         make_identity(nc, ident[:])
@@ -108,14 +107,6 @@ def tile_swintransformerblock_pa_kernel(
 
         def out_scale(n):
             return Q_SCALE if n * BANK < CHANNELS else 1.0
-
-        bias = const.tile([P, OUT_COLS], F32)
-
-        def spread_bias(n):
-            cols = slice(n * BANK, (n + 1) * BANK)
-            spread = psum.tile([P, BANK], F32, tag="bank")
-            nc.tensor.matmul(out=spread[:], lhsT=ones[:], rhs=b_rows[:, cols], start=True, stop=True)
-            nc.scalar.mul(out=bias[:, cols], in_=spread[:], mul=out_scale(n))
 
         h_codes = keep.tile([P, PASSES, TOKENS], U32, align_bytes=64)
         h_scales = keep.tile([P, PASSES, TOKENS], U8, align_bytes=64)
@@ -174,7 +165,8 @@ def tile_swintransformerblock_pa_kernel(
             rows = slice(half * BANK, (half + 1) * BANK)
             grouped = group_h.tile([P, BANK, PACK], BF16, align_bytes=64, tag="grouped_h")
             nc.vector.tensor_copy(
-                out=grouped[:], in_=planes[half][:, PACK * g : PACK * (g + 1), :].rearrange("p t c -> p c t")
+                out=grouped[:].rearrange("p (c i) t -> p c t i", i=4),
+                in_=planes[half][:, PACK * g : PACK * (g + 1), :].rearrange("p t (c i) -> p c t i", i=4),
             )
             nc.vector.quantize_mx(
                 out=h_codes[:, g, rows].bitcast(FP8X4),
@@ -212,16 +204,14 @@ def tile_swintransformerblock_pa_kernel(
 
         result_of = {}
 
-        def project(half, n):
-            cols = slice(n * BANK, (n + 1) * BANK)
-            which, part = divmod(n, CHANNELS // BANK)
-            part_cols = slice(part * BANK, (part + 1) * BANK)
-            accs = [psum.tile([P, BANK], F32, name="acc", tag="bank") for i in range(HALF_TILES)]
+        def project(row_blocks, col_blocks):
+            pairs = [(m, n) for m in row_blocks for n in col_blocks]
+            accs = [psum.tile([P, BANK], F32, name="acc", tag="bank") for pair in pairs]
             for g in range(PASSES):
-                for i in range(HALF_TILES):
-                    rows = slice((half * HALF_TILES + i) * P, (half * HALF_TILES + i + 1) * P)
+                for acc, (m, n) in zip(accs, pairs):
+                    rows = slice(m * P, (m + 1) * P)
                     nc.tensor.matmul_mx(
-                        out=accs[i][:],
+                        out=acc[:],
                         lhsT=h_codes[:, g, rows].bitcast(FP8X4),
                         lhsT_scale=h_scales[:, g, rows],
                         rhs=w_codes[:, n, g, :].bitcast(FP8X4),
@@ -229,26 +219,26 @@ def tile_swintransformerblock_pa_kernel(
                         start=(g == 0),
                         stop=(g == PASSES - 1),
                     )
-            for i in range(HALF_TILES):
-                m = half * HALF_TILES + i
+            for j, (m, n) in enumerate(pairs):
+                part = n % PARTS
                 if part == 0:
                     result_of[m] = results.tile([P, CHANNELS], F32, name="result", tag="result")
-                result = result_of[m][:, part_cols]
-                if (n * HALF_TILES + i) % 3 == 2:
-                    nc.scalar.mul(out=result, in_=accs[i][:], mul=out_scale(n))
+                result = result_of[m][:, part * BANK : (part + 1) * BANK]
+                cols = slice(n * BANK, (n + 1) * BANK)
+                if j == 0:
+                    nc.scalar.mul(out=result, in_=accs[j][:], mul=out_scale(n))
                     nc.gpsimd.tensor_tensor(out=result, in0=result, in1=bias[:, cols], op=ALU.add)
                 else:
                     nc.vector.scalar_tensor_tensor(
-                        out=result, in0=accs[i][:], scalar=out_scale(n), in1=bias[:, cols], op0=ALU.mult, op1=ALU.add
+                        out=result, in0=accs[j][:], scalar=out_scale(n), in1=bias[:, cols], op0=ALU.mult, op1=ALU.add
                     )
-                if part == CHANNELS // BANK - 1:
-                    nc.sync.dma_start(out=out_rows[which][m * P : (m + 1) * P, :], in_=result_of[m][:])
+            complete = [(m, n // PARTS) for m, n in pairs if n % PARTS == PARTS - 1]
+            for m, which in complete[1:] + complete[:1]:
+                nc.sync.dma_start(out=out_rows[which][m * P : (m + 1) * P, :], in_=result_of[m][:])
 
         for i in range(HALF_TILES):
             tile_stats(source_tile(0, i))
             tile_norm(source_tile(0, i))
-            for n in range(2 * i, min(2 * i + 2, W_BLOCKS)):
-                spread_bias(n)
         turn_w(0)
         tile_stats(source_tile(1, 0))
         tile_stats(source_tile(1, 1))
@@ -260,21 +250,29 @@ def tile_swintransformerblock_pa_kernel(
         quantise_h(0, 0)
         turn_h(0, 1)
         tile_norm(source_tile(1, 2))
+        nc.gpsimd.tensor_scalar(
+            out=bias[:, 0:CHANNELS], in0=bias[:, 0:CHANNELS], scalar1=Q_SCALE, scalar2=0.0, op0=ALU.mult, op1=ALU.add
+        )
         quantise_h(0, 1)
         turn_w(1)
         quantise_w(1)
         turn_w(2)
-        project(0, 0)
-        quantise_w(2)
-        tile_stats(source_tile(1, 3))
-        tile_norm(source_tile(1, 3))
-        for n in range(3, W_BLOCKS):
-            turn_w(n)
-            quantise_w(n)
-            project(0, n - 2)
-        for g in range(PASSES):
-            turn_h(1, g)
-            quantise_h(1, g)
-            project(0, W_BLOCKS - PASSES + g)
-        for n in range(W_BLOCKS):
-            project(1, n)
+        rounds = [(which, m) for which in range(OUT_COLS // CHANNELS) for m in range(0, HALF_TILES, 2)]
+        later = [("w", 3), ("w", 4), ("w", 5), ("h", 0), ("h", 1)]
+        for i, (which, m) in enumerate(rounds):
+            project([m, m + 1], [PARTS * which, PARTS * which + 1])
+            if i == 0:
+                quantise_w(2)
+                tile_stats(source_tile(1, 3))
+                tile_norm(source_tile(1, 3))
+            if i < len(later):
+                kind, k = later[i]
+                if kind == "w":
+                    turn_w(k)
+                    quantise_w(k)
+                else:
+                    turn_h(1, k)
+                    quantise_h(1, k)
+        for which in range(OUT_COLS // CHANNELS):
+            for m in range(HALF_TILES, X_TILES, 2):
+                project([m, m + 1], [PARTS * which, PARTS * which + 1])

from contextlib import ExitStack

import concourse.mybir as mybir
from concourse.masks import make_identity

F32 = mybir.dt.float32
BF16 = mybir.dt.bfloat16
U32 = mybir.dt.uint32
U8 = mybir.dt.uint8
FP8X4 = mybir.dt.float8_e4m3fn_x4
ALU = mybir.AluOpType
ACT = mybir.ActivationFunctionType

P = 128
TOKENS = 1024
CHANNELS = 1024
OUT_COLS = 3072
GRID = 32
SHIFT = 4
WINDOW = 8
WINDOWS_IN_ROW = GRID // WINDOW
GRID_ROWS_IN_TILE = P // GRID
EPS = 1e-5
Q_SCALE = 64 ** -0.5

PACK = 4
K_PASS = P * PACK
PASSES = CHANNELS // K_PASS
BANK = 512
W_BLOCKS = OUT_COLS // BANK
W_TILES = BANK // P
X_TILES = TOKENS // P
HALVES = 2
HALF_TILES = X_TILES // HALVES
PLANES = CHANNELS // P
BN_CHUNK = 512
PARTS = CHANNELS // BANK

FLOPS = 2 * TOKENS * CHANNELS * OUT_COLS


def tile_swintransformerblock_pa_kernel(
    tc, x, ln1_w, ln1_b, in_proj_w, in_proj_b, out_0, out_1, out_2
):
    nc = tc.nc
    x_rows = x.flatten_outer_dims()
    out_rows = [o.rearrange("w n h d -> (w n) (h d)") for o in (out_0, out_1, out_2)]

    with ExitStack() as stack:
        const = stack.enter_context(tc.tile_pool(name="const", bufs=1))
        keep = stack.enter_context(tc.tile_pool(name="keep", bufs=1))
        small = stack.enter_context(tc.tile_pool(name="small", bufs=X_TILES))
        normed = stack.enter_context(tc.tile_pool(name="normed", bufs=6))
        group_h = stack.enter_context(tc.tile_pool(name="group_h", bufs=2))
        group_w = stack.enter_context(tc.tile_pool(name="group_w", bufs=4))
        results = stack.enter_context(tc.tile_pool(name="results", bufs=8))
        psum = stack.enter_context(tc.psum_pool(name="psum", bufs=8))

        x_sb = [keep.tile([P, CHANNELS], BF16, name="x_sb%d" % s) for s in range(X_TILES)]
        w_raw = [keep.tile([P, W_TILES, CHANNELS], BF16, name="w_raw%d" % n) for n in range(W_BLOCKS)]

        def source_tile(half, i):
            return (half * HALF_TILES + i + 1) % X_TILES

        def load_x(half):
            for i in range(HALF_TILES):
                s = source_tile(half, i)
                nc.sync.dma_start(out=x_sb[s][:], in_=x_rows[s * P : (s + 1) * P, :])

        def load_w(n):
            rows = in_proj_w[n * BANK : (n + 1) * BANK, :]
            nc.sync.dma_start(out=w_raw[n][:], in_=rows.rearrange("(a p) k -> p a k", p=P))

        ln_gain_bf = const.tile([P, PLANES // 2, 2], BF16)
        ln_bias_bf = const.tile([P, PLANES // 2, 2], BF16)
        nc.scalar.dma_start(out=ln_gain_bf[:], in_=ln1_w.rearrange("(r p e) -> p r e", p=P, e=2))
        nc.scalar.dma_start(out=ln_bias_bf[:], in_=ln1_b.rearrange("(r p e) -> p r e", p=P, e=2))

        load_x(0)
        load_w(0)
        load_x(1)
        load_w(1)
        load_w(2)
        bias = const.tile([P, OUT_COLS], BF16)
        nc.sync.dma_start(out=bias[:], in_=in_proj_b.partition_broadcast(P))
        for n in range(3, W_BLOCKS):
            load_w(n)

        eps = const.tile([P, 1], F32)
        eps_rsqrt = const.tile([P, 1], F32)
        nc.vector.memset(eps[:], EPS)
        nc.scalar.activation(out=eps_rsqrt[:], in_=eps[:], func=ACT.Abs_reciprocal_sqrt)

        ident = const.tile([P, P], F32)
        make_identity(nc, ident[:])
        ident_rows = ident[:].rearrange("p (i j) -> p i j", j=GRID)
        rotated = const.tile([P, GRID_ROWS_IN_TILE, GRID], F32)
        nc.vector.tensor_copy(out=rotated[:, :, 0 : GRID - SHIFT], in_=ident_rows[:, :, SHIFT:GRID])
        nc.vector.tensor_copy(out=rotated[:, :, GRID - SHIFT : GRID], in_=ident_rows[:, :, 0:SHIFT])
        perm = const.tile([P, WINDOWS_IN_ROW, GRID_ROWS_IN_TILE, WINDOW], F32)
        nc.vector.tensor_copy(out=perm[:], in_=rotated[:].rearrange("p i (w c) -> p w i c", c=WINDOW))
        perm_2d = perm[:].rearrange("p w i c -> p (w i c)")
        ln_gain = const.tile([P, PLANES // 2, 2], F32)
        ln_bias = const.tile([P, PLANES // 2, 2], F32)
        nc.gpsimd.tensor_copy(out=ln_gain[:], in_=ln_gain_bf[:])
        nc.gpsimd.tensor_copy(out=ln_bias[:], in_=ln_bias_bf[:])

        def out_scale(n):
            return Q_SCALE if n * BANK < CHANNELS else 1.0

        h_codes = keep.tile([P, PASSES, TOKENS], U32, align_bytes=64)
        h_scales = keep.tile([P, PASSES, TOKENS], U8, align_bytes=64)
        w_codes = keep.tile([P, W_BLOCKS, PASSES, BANK], U32, align_bytes=64)
        w_scales = keep.tile([P, W_BLOCKS, PASSES, BANK], U8, align_bytes=64)
        planes = [keep.tile([P, PLANES, BANK], BF16, name="planes%d" % h) for h in range(HALVES)]
        mean_var = {}
        neg_mean = {}
        xn = {}
        grouped_w = {}

        def tile_stats(s):
            stats = small.tile([P, CHANNELS // BN_CHUNK, 6], F32, tag="stats")
            for c in range(CHANNELS // BN_CHUNK):
                nc.vector.bn_stats(out=stats[:, c, :], in_=x_sb[s][:, c * BN_CHUNK : (c + 1) * BN_CHUNK])
            mean_var[s] = small.tile([P, 2], F32, name="mean_var", tag="mean_var")
            nc.vector.bn_aggr(out=mean_var[s][:], in_=stats[:].rearrange("p c s -> p (c s)"))
            neg_mean[s] = small.tile([P, 1], F32, name="neg_mean", tag="neg_mean")
            nc.vector.tensor_scalar_mul(out=neg_mean[s][:], in0=mean_var[s][:, 0:1], scalar1=-1.0)

        def tile_norm(s):
            rstd = small.tile([P, 1], F32, tag="rstd")
            nc.scalar.activation(
                out=rstd[:], in_=mean_var[s][:, 1:2], func=ACT.Abs_reciprocal_sqrt, bias=eps[:, 0:1]
            )
            xn[s] = normed.tile([P, 2, CHANNELS // 2], F32, name="xn", tag="xn")
            nc.gpsimd.tensor_scalar(
                out=xn[s][:],
                in0=x_sb[s][:].rearrange("p (w e) -> p e w", e=2),
                scalar1=neg_mean[s][:, 0:1],
                scalar2=rstd[:, 0:1],
                op0=ALU.add,
                op1=ALU.mult,
            )

        def turn_h(half, g):
            for t in range(PACK):
                r, e = divmod(PACK * g + t, 2)
                turned = psum.tile([P, 2, WINDOWS_IN_ROW, 2, P // WINDOWS_IN_ROW], F32, tag="bank")
                for i in range(HALF_TILES):
                    wr, hb = divmod(i, 2)
                    nc.tensor.transpose(
                        out=turned[:, wr, :, hb, :],
                        in_=xn[source_tile(half, i)][:, e, r * P : (r + 1) * P],
                        identity=perm_2d,
                    )
                nc.scalar.activation(
                    out=planes[half][:, PACK * g + t, :],
                    in_=turned[:].rearrange("p a w b c -> p (a w b c)"),
                    func=ACT.Identity,
                    scale=ln_gain[:, r, e : e + 1],
                    bias=ln_bias[:, r, e : e + 1],
                )

        def quantise_h(half, g):
            rows = slice(half * BANK, (half + 1) * BANK)
            grouped = group_h.tile([P, BANK, PACK], BF16, align_bytes=64, tag="grouped_h")
            nc.vector.tensor_copy(
                out=grouped[:].rearrange("p (c i) t -> p c t i", i=4),
                in_=planes[half][:, PACK * g : PACK * (g + 1), :].rearrange("p t (c i) -> p c t i", i=4),
            )
            nc.vector.quantize_mx(
                out=h_codes[:, g, rows].bitcast(FP8X4),
                scales=h_scales[:, g, rows],
                in_=grouped[:].rearrange("p c t -> p (c t)"),
            )

        def turn_w(n):
            words = w_raw[n][:].bitcast(F32)
            for g in range(PASSES):
                grouped_w[n, g] = group_w.tile([P, BANK, PACK], BF16, align_bytes=64, name="grouped_w", tag="grouped_w")
                grouped_words = grouped_w[n, g][:].bitcast(F32)
                for pair in range(W_TILES // 2):
                    turned = psum.tile([P, 2, 2, P], F32, tag="bank")
                    for u in range(2):
                        for a2 in range(2):
                            first = (2 * g + u) * P
                            nc.tensor.transpose(
                                out=turned[:, u, a2, :],
                                in_=words[:, 2 * pair + a2, first : first + P],
                                identity=ident[:],
                            )
                    nc.scalar.copy(
                        out=grouped_words[:, 2 * pair * P : 2 * (pair + 1) * P, :],
                        in_=turned[:].rearrange("p u a c -> p (a c) u"),
                    )

        def quantise_w(n):
            for g in range(PASSES):
                nc.vector.quantize_mx(
                    out=w_codes[:, n, g, :].bitcast(FP8X4),
                    scales=w_scales[:, n, g, :],
                    in_=grouped_w[n, g][:].rearrange("p c t -> p (c t)"),
                )

        result_of = {}

        def project(row_blocks, col_blocks):
            pairs = [(m, n) for m in row_blocks for n in col_blocks]
            accs = [psum.tile([P, BANK], F32, name="acc", tag="bank") for pair in pairs]
            for g in range(PASSES):
                for acc, (m, n) in zip(accs, pairs):
                    rows = slice(m * P, (m + 1) * P)
                    nc.tensor.matmul_mx(
                        out=acc[:],
                        lhsT=h_codes[:, g, rows].bitcast(FP8X4),
                        lhsT_scale=h_scales[:, g, rows],
                        rhs=w_codes[:, n, g, :].bitcast(FP8X4),
                        rhs_scale=w_scales[:, n, g, :],
                        start=(g == 0),
                        stop=(g == PASSES - 1),
                    )
            for j, (m, n) in enumerate(pairs):
                part = n % PARTS
                if part == 0:
                    result_of[m] = results.tile([P, CHANNELS], F32, name="result", tag="result")
                result = result_of[m][:, part * BANK : (part + 1) * BANK]
                cols = slice(n * BANK, (n + 1) * BANK)
                if j == 0:
                    nc.scalar.mul(out=result, in_=accs[j][:], mul=out_scale(n))
                    nc.gpsimd.tensor_tensor(out=result, in0=result, in1=bias[:, cols], op=ALU.add)
                else:
                    nc.vector.scalar_tensor_tensor(
                        out=result, in0=accs[j][:], scalar=out_scale(n), in1=bias[:, cols], op0=ALU.mult, op1=ALU.add
                    )
            complete = [(m, n // PARTS) for m, n in pairs if n % PARTS == PARTS - 1]
            for m, which in complete[1:] + complete[:1]:
                nc.sync.dma_start(out=out_rows[which][m * P : (m + 1) * P, :], in_=result_of[m][:])

        for i in range(HALF_TILES):
            tile_stats(source_tile(0, i))
            tile_norm(source_tile(0, i))
        turn_w(0)
        tile_stats(source_tile(1, 0))
        tile_stats(source_tile(1, 1))
        quantise_w(0)
        turn_h(0, 0)
        tile_norm(source_tile(1, 0))
        tile_norm(source_tile(1, 1))
        tile_stats(source_tile(1, 2))
        quantise_h(0, 0)
        turn_h(0, 1)
        tile_norm(source_tile(1, 2))
        nc.gpsimd.tensor_scalar(
            out=bias[:, 0:CHANNELS], in0=bias[:, 0:CHANNELS], scalar1=Q_SCALE, scalar2=0.0, op0=ALU.mult, op1=ALU.add
        )
        quantise_h(0, 1)
        turn_w(1)
        quantise_w(1)
        turn_w(2)
        rounds = [(which, m) for which in range(OUT_COLS // CHANNELS) for m in range(0, HALF_TILES, 2)]
        later = [("w", 3), ("w", 4), ("w", 5), ("h", 0), ("h", 1)]
        for i, (which, m) in enumerate(rounds):
            project([m, m + 1], [PARTS * which, PARTS * which + 1])
            if i == 0:
                quantise_w(2)
                tile_stats(source_tile(1, 3))
                tile_norm(source_tile(1, 3))
            if i < len(later):
                kind, k = later[i]
                if kind == "w":
                    turn_w(k)
                    quantise_w(k)
                else:
                    turn_h(1, k)
                    quantise_h(1, k)
        for which in range(OUT_COLS // CHANNELS):
            for m in range(HALF_TILES, X_TILES, 2):
                project([m, m + 1], [PARTS * which, PARTS * which + 1])
